import numpy as np
import ml_dtypes


def mxq(x, axis, fmt="e4m3"):
    dtype, down = {"e4m3": (ml_dtypes.float8_e4m3fn, 7), "e5m2": (ml_dtypes.float8_e5m2, 14)}[fmt]
    v = np.moveaxis(np.asarray(x, np.float32).astype(ml_dtypes.bfloat16).astype(np.float64), axis, -1)
    blocks = v.reshape(v.shape[:-1] + (-1, 32))
    amax = np.abs(blocks).max(-1, keepdims=True)
    byte = np.maximum(np.where(amax > 0, np.frexp(amax)[1] - 1 + 127, 0) - down, 1)
    scale = np.exp2(byte - 127.0)
    codes = (blocks / scale).astype(np.float32).astype(dtype).astype(np.float64)
    return np.moveaxis((codes * scale).reshape(v.shape), -1, axis)


WIDE = False


def mx_kscale(k):
    if not WIDE:
        return np.ones(k)
    levels = np.array([10, -10, 5, -5, 0])
    a = np.random.permutation(np.resize(levels, k // 512 * 4)).reshape(k // 512, 4)
    idx = np.arange(k)
    return np.exp2(a[idx // 512, idx % 128 // 32])


BF16 = ml_dtypes.bfloat16


def bf(x):
    return np.asarray(x, np.float32).astype(BF16)


def f64(x):
    return np.asarray(x).astype(np.float64)


B, CIN, R, COUT, H, W, D, KS = 1, 512, 512, 512, 6, 8, 8, 3
P = H * W * D
PAD = (KS - 1) // 2


def slice_in_dim(t, a, b, axis):
    idx = [slice(None)] * t.ndim
    idx[axis] = slice(a, b)
    return t[tuple(idx)]


def axis_contract(t, U, axis):
    L = t.shape[axis] - (KS - 1)
    rshape = (1, U.shape[1], 1, 1, 1)
    acc = slice_in_dim(t, 0, L, axis) * U[0].reshape(rshape)
    for k in range(1, KS):
        acc = acc + slice_in_dim(t, k, k + L, axis) * U[k].reshape(rshape)
    return acc


def setup_inputs():
    s, t = mx_kscale(CIN), mx_kscale(R)
    return {"x": bf(np.random.standard_normal((B, CIN, H, W, D)) * s[None, :, None, None, None]),
            "U_kh": bf(np.random.standard_normal((KS, R)) / np.sqrt(KS)),
            "U_kw": bf(np.random.standard_normal((KS, R)) / np.sqrt(KS)),
            "U_kd": bf(np.random.standard_normal((KS, R)) / np.sqrt(KS)),
            "U_c_in": bf(np.random.standard_normal((CIN, R)) / np.sqrt(CIN) / s[:, None] * t[None, :]),
            "U_c_out": bf(np.random.standard_normal((R, COUT)) / np.sqrt(R) / t[:, None]),
            "bias": bf(np.random.standard_normal(COUT) * 0.5)}


def reference(x, U_kh, U_kw, U_kd, U_c_in, U_c_out, bias):
    xq = mxq(f64(x), 1, "e4m3").reshape(B, CIN, P)
    y = (mxq(f64(U_c_in), 0, "e4m3").T @ xq).reshape(B, R, H, W, D)
    y = np.pad(y, ((0, 0), (0, 0), (PAD, PAD), (PAD, PAD), (PAD, PAD)))
    y = axis_contract(y, f64(U_kh), 2)
    y = axis_contract(y, f64(U_kw), 3)
    y = axis_contract(y, f64(U_kd), 4)
    out = (mxq(f64(U_c_out), 0, "e4m3").T @ mxq(y, 1, "e4m3").reshape(B, R, P)).reshape(B, COUT, H, W, D)
    return out + f64(bias)[None, :, None, None, None]

@@ -1,0 +1,196 @@
+from contextlib import ExitStack
+
+import concourse.mybir as mybir
+from concourse.masks import make_identity
+
+F32 = mybir.dt.float32
+BF16 = mybir.dt.bfloat16
+U32 = mybir.dt.uint32
+U8 = mybir.dt.uint8
+FP8X4 = mybir.dt.float8_e4m3fn_x4
+MULT = mybir.AluOpType.mult
+ADD = mybir.AluOpType.add
+COPY = mybir.ActivationFunctionType.Copy
+IDENTITY = mybir.ActivationFunctionType.Identity
+
+P = 128
+PACK = 4
+CH = P * PACK
+H, W, D = 6, 8, 8
+POS = H * W * D
+TAPS = 3
+TILES = CH // P
+CHUNKS = ((0, 256), (256, 384))
+
+FLOPS = 2 * (2 * CH * CH * POS) + 3 * (2 * TAPS - 1) * CH * POS + CH * POS
+
+
+def regroup(engine_copy, grouped, rows, lo, hi):
+    engine_copy(
+        out=grouped[:, lo:hi, :].rearrange("p (c i) j -> p c j i", i=4),
+        in_=rows[:, :, lo:hi].rearrange("p j (c i) -> p c j i", i=4),
+    )
+
+
+def quantise(nc, codes, scales, grouped, lo, hi):
+    nc.vector.quantize_mx(
+        out=codes[:, lo:hi].bitcast(FP8X4),
+        scales=scales[:, lo:hi],
+        in_=grouped[:, lo:hi, :].rearrange("p c j -> p (c j)"),
+    )
+
+
+def tile_lowrankconv3d_s_kernel(tc, x, U_kh, U_kw, U_kd, U_c_in, U_c_out, bias, out):
+    nc = tc.nc
+    x_rows = x.rearrange("b c h w d -> (b c) (h w d)")
+    out_rows = out.rearrange("b o h w d -> (b o) (h w d)")
+
+    with ExitStack() as stack:
+        keep = stack.enter_context(tc.tile_pool(name="keep", bufs=1))
+        psum = stack.enter_context(tc.psum_pool(name="psum", bufs=8))
+
+        x_raw = keep.tile([P, PACK, POS], BF16)
+        uin_raw = keep.tile([P, PACK, CH], BF16)
+        uout_raw = keep.tile([P, PACK, CH], BF16)
+        nc.sync.dma_start(out=x_raw[:], in_=x_rows.rearrange("(p j) n -> p j n", j=PACK))
+        uin_view = U_c_in.rearrange("(p j) r -> p j r", j=PACK)
+        half = CH // 2
+        nc.sync.dma_start(out=uin_raw[:, :, 0:half], in_=uin_view[:, :, 0:half])
+        nc.sync.dma_start(out=uin_raw[:, :, half:CH], in_=uin_view[:, :, half:CH])
+        nc.sync.dma_start(out=uout_raw[:], in_=U_c_out.rearrange("(t p) o -> p t o", p=P))
+
+        par_rows = keep.tile([P, P], BF16)
+        nc.vector.memset(par_rows[:], 0.0)
+        for f, taps in enumerate((U_kh, U_kw, U_kd)):
+            nc.scalar.dma_start(
+                out=par_rows[f * TAPS * TILES : (f + 1) * TAPS * TILES, :],
+                in_=taps.rearrange("k (t p) -> (k t) p", p=P),
+            )
+        bias_row = 3 * TAPS * TILES
+        nc.scalar.dma_start(
+            out=par_rows[bias_row : bias_row + TILES, :], in_=bias.rearrange("(t p) -> t p", p=P)
+        )
+        ident = keep.tile([P, P], BF16)
+        make_identity(nc, ident[:])
+        par_ps = psum.tile([P, P], BF16, tag="bank")
+        nc.tensor.transpose(par_ps[:], par_rows[:], ident[:])
+        par = keep.tile([P, bias_row + TILES], F32)
+        nc.scalar.activation(out=par[:], in_=par_ps[:, 0 : bias_row + TILES], func=COPY)
+
+        def tap(f, k, t):
+            col = (f * TAPS + k) * TILES + t
+            return par[:, col : col + 1]
+
+        x_grp = keep.tile([P, POS, PACK], BF16, align_bytes=64)
+        x_codes = keep.tile([P, POS], U32, align_bytes=64)
+        x_scales = keep.tile([P, POS], U8, align_bytes=64)
+        uin_grp = keep.tile([P, CH, PACK], BF16, align_bytes=64)
+        uin_codes = keep.tile([P, CH], U32, align_bytes=64)
+        uin_scales = keep.tile([P, CH], U8, align_bytes=64)
+        regroup(nc.vector.tensor_copy, x_grp, x_raw, 0, 256)
+        regroup(nc.scalar.copy, x_grp, x_raw, 256, 384)
+        regroup(nc.vector.tensor_copy, uin_grp, uin_raw, 0, half)
+        regroup(nc.scalar.copy, uin_grp, uin_raw, half, CH)
+        quantise(nc, x_codes, x_scales, x_grp, 0, 256)
+        quantise(nc, x_codes, x_scales, x_grp, 256, 384)
+        quantise(nc, uin_codes, uin_scales, uin_grp, 0, half)
+        quantise(nc, uin_codes, uin_scales, uin_grp, half, CH)
+
+        y0 = []
+        for t in range(TILES):
+            bank = psum.tile([P, 512], F32, tag="bank", name="y0_%d" % t)
+            for lo, hi in CHUNKS:
+                nc.tensor.matmul_mx(
+                    out=bank[:, lo:hi],
+                    lhsT=uin_codes[:, t * P : (t + 1) * P].bitcast(FP8X4),
+                    lhsT_scale=uin_scales[:, t * P : (t + 1) * P],
+                    rhs=x_codes[:, lo:hi].bitcast(FP8X4),
+                    rhs_scale=x_scales[:, lo:hi],
+                    start=True,
+                    stop=True,
+                )
+            y0.append(bank)
+
+        uout_grp = keep.tile([P, CH, PACK], BF16, align_bytes=64)
+        uout_codes = keep.tile([P, CH], U32, align_bytes=64)
+        uout_scales = keep.tile([P, CH], U8, align_bytes=64)
+        for t in range(TILES):
+            regroup(nc.scalar.copy, uout_grp, uout_raw, t * P, (t + 1) * P)
+        quantise(nc, uout_codes, uout_scales, uout_grp, 0, CH)
+
+        y1 = keep.tile([P, TILES, POS], F32)
+        y2 = keep.tile([P, TILES, POS], F32)
+        side = keep.tile([P, TILES, POS], F32)
+        y3 = keep.tile([P, TILES, POS], BF16)
+        nc.vector.memset(side[:].rearrange("p t (m d) -> p (t m) d", d=D)[:, :, 0:1], 0.0)
+
+        def add_tap(acc, src, coef):
+            nc.vector.scalar_tensor_tensor(out=acc, in0=src, scalar=coef, in1=acc, op0=MULT, op1=ADD)
+
+        step = W * D
+        for t in range(TILES):
+            nc.scalar.activation(out=y1[:, t, :], in_=y0[t][:, 0:POS], func=COPY, scale=tap(0, 1, t))
+        for t in range(TILES):
+            add_tap(y1[:, t, step:POS], y0[t][:, 0 : POS - step], tap(0, 0, t))
+        for t in range(TILES):
+            add_tap(y1[:, t, 0 : POS - step], y0[t][:, step:POS], tap(0, 2, t))
+
+        for t in range(TILES):
+            nc.scalar.activation(out=y2[:, t, :], in_=y1[:, t, :], func=COPY, scale=tap(1, 1, t))
+        for t in range(TILES):
+            src = y1[:, t, :].rearrange("p (h n) -> p h n", n=step)
+            acc = y2[:, t, :].rearrange("p (h n) -> p h n", n=step)
+            add_tap(acc[:, :, D:step], src[:, :, 0 : step - D], tap(1, 0, t))
+        for t in range(TILES):
+            src = y1[:, t, :].rearrange("p (h n) -> p h n", n=step)
+            acc = y2[:, t, :].rearrange("p (h n) -> p h n", n=step)
+            add_tap(acc[:, :, 0 : step - D], src[:, :, D:step], tap(1, 2, t))
+
+        y3_grp = keep.tile([P, POS, PACK], BF16, align_bytes=64)
+        y3_codes = keep.tile([P, POS], U32, align_bytes=64)
+        y3_scales = keep.tile([P, POS], U8, align_bytes=64)
+        res = keep.tile([P, TILES, POS], F32)
+        o_ps = [psum.tile([P, 512], F32, tag="bank", name="o_%d" % t) for t in range(TILES)]
+        out_view = out_rows.rearrange("(t p) n -> p t n", p=P)
+        for lo, hi in CHUNKS:
+            for t in range(TILES):
+                src = y2[:, t, lo:hi].rearrange("p (m d) -> p m d", d=D)
+                acc = side[:, t, lo:hi].rearrange("p (m d) -> p m d", d=D)
+                nc.scalar.activation(
+                    out=acc[:, :, 1:D], in_=src[:, :, 0 : D - 1], func=COPY, scale=tap(2, 0, t)
+                )
+            for t in range(TILES):
+                src = y2[:, t, lo:hi].rearrange("p (m d) -> p m d", d=D)
+                acc = side[:, t, lo:hi].rearrange("p (m d) -> p m d", d=D)
+                add_tap(acc[:, :, 0 : D - 1], src[:, :, 1:D], tap(2, 2, t))
+            for t in range(TILES):
+                nc.vector.scalar_tensor_tensor(
+                    out=y3[:, t, lo:hi],
+                    in0=y2[:, t, lo:hi],
+                    scalar=tap(2, 1, t),
+                    in1=side[:, t, lo:hi],
+                    op0=MULT,
+                    op1=ADD,
+                )
+            last = hi == POS
+            regroup(nc.vector.tensor_copy if last else nc.scalar.copy, y3_grp, y3, lo, hi)
+            quantise(nc, y3_codes, y3_scales, y3_grp, lo, hi)
+            for t in range(TILES):
+                nc.tensor.matmul_mx(
+                    out=o_ps[t][:, lo:hi],
+                    lhsT=uout_codes[:, t * P : (t + 1) * P].bitcast(FP8X4),
+                    lhsT_scale=uout_scales[:, t * P : (t + 1) * P],
+                    rhs=y3_codes[:, lo:hi].bitcast(FP8X4),
+                    rhs_scale=y3_scales[:, lo:hi],
+                    start=True,
+                    stop=True,
+                )
+            for t in range(TILES):
+                bias_t = par[:, bias_row + t : bias_row + t + 1]
+                if t % 2 == 0 or not last:
+                    nc.scalar.activation(
+                        out=res[:, t, lo:hi], in_=o_ps[t][:, lo:hi], func=IDENTITY, bias=bias_t
+                    )
+                else:
+                    nc.vector.tensor_scalar_add(out=res[:, t, lo:hi], in0=o_ps[t][:, lo:hi], scalar1=bias_t)
+            nc.sync.dma_start(out=out_view[:, :, lo:hi], in_=res[:, :, lo:hi])

@@ -21,6 +21,7 @@ POS = H * W * D
 TAPS = 3
 TILES = CH // P
 CHUNKS = ((0, 256), (256, 384))
+PAIRS = ((0, 1), (2, 3))
 
 FLOPS = 2 * (2 * CH * CH * POS) + 3 * (2 * TAPS - 1) * CH * POS + CH * POS
 
@@ -40,6 +41,18 @@ def quantise(nc, codes, scales, grouped, lo, hi):
     )
 
 
+def product(nc, bank, w_codes, w_scales, t, m_codes, m_scales, lo, hi):
+    nc.tensor.matmul_mx(
+        out=bank[:, lo:hi],
+        lhsT=w_codes[:, t * P : (t + 1) * P].bitcast(FP8X4),
+        lhsT_scale=w_scales[:, t * P : (t + 1) * P],
+        rhs=m_codes[:, lo:hi].bitcast(FP8X4),
+        rhs_scale=m_scales[:, lo:hi],
+        start=True,
+        stop=True,
+    )
+
+
 def tile_lowrankconv3d_s_kernel(tc, x, U_kh, U_kw, U_kd, U_c_in, U_c_out, bias, out):
     nc = tc.nc
     x_rows = x.rearrange("b c h w d -> (b c) (h w d)")
@@ -48,6 +61,7 @@ def tile_lowrankconv3d_s_kernel(tc, x, U_kh, U_kw, U_kd, U_c_in, U_c_out, bias, 
     with ExitStack() as stack:
         keep = stack.enter_context(tc.tile_pool(name="keep", bufs=1))
         psum = stack.enter_context(tc.psum_pool(name="psum", bufs=8))
+        stack.enter_context(tc.manual_schedule())
 
         x_raw = keep.tile([P, PACK, POS], BF16)
         uin_raw = keep.tile([P, PACK, CH], BF16)
@@ -81,6 +95,12 @@ def tile_lowrankconv3d_s_kernel(tc, x, U_kh, U_kw, U_kd, U_c_in, U_c_out, bias, 
             col = (f * TAPS + k) * TILES + t
             return par[:, col : col + 1]
 
+        y1 = keep.tile([P, TILES, POS], F32)
+        y2 = keep.tile([P, TILES, POS], F32)
+        side = keep.tile([P, TILES, POS], F32)
+        y3 = keep.tile([P, TILES, POS], BF16)
+        nc.vector.memset(side[:].rearrange("p t (m d) -> p (t m) d", d=D)[:, :, 0:1], 0.0)
+
         x_grp = keep.tile([P, POS, PACK], BF16, align_bytes=64)
         x_codes = keep.tile([P, POS], U32, align_bytes=64)
         x_scales = keep.tile([P, POS], U8, align_bytes=64)
@@ -93,76 +113,69 @@ def tile_lowrankconv3d_s_kernel(tc, x, U_kh, U_kw, U_kd, U_c_in, U_c_out, bias, 
         regroup(nc.scalar.copy, uin_grp, uin_raw, half, CH)
         quantise(nc, x_codes, x_scales, x_grp, 0, 256)
         quantise(nc, x_codes, x_scales, x_grp, 256, 384)
-        quantise(nc, uin_codes, uin_scales, uin_grp, 0, half)
-        quantise(nc, uin_codes, uin_scales, uin_grp, half, CH)
-
-        y0 = []
-        for t in range(TILES):
-            bank = psum.tile([P, 512], F32, tag="bank", name="y0_%d" % t)
-            for lo, hi in CHUNKS:
-                nc.tensor.matmul_mx(
-                    out=bank[:, lo:hi],
-                    lhsT=uin_codes[:, t * P : (t + 1) * P].bitcast(FP8X4),
-                    lhsT_scale=uin_scales[:, t * P : (t + 1) * P],
-                    rhs=x_codes[:, lo:hi].bitcast(FP8X4),
-                    rhs_scale=x_scales[:, lo:hi],
-                    start=True,
-                    stop=True,
-                )
-            y0.append(bank)
+        y0 = [psum.tile([P, 512], F32, tag="bank", name="y0_%d" % t) for t in range(TILES)]
+        for pair in PAIRS:
+            quantise(nc, uin_codes, uin_scales, uin_grp, pair[0] * P, (pair[1] + 1) * P)
+            for t in pair:
+                for lo, hi in CHUNKS:
+                    product(nc, y0[t], uin_codes, uin_scales, t, x_codes, x_scales, lo, hi)
 
         uout_grp = keep.tile([P, CH, PACK], BF16, align_bytes=64)
         uout_codes = keep.tile([P, CH], U32, align_bytes=64)
         uout_scales = keep.tile([P, CH], U8, align_bytes=64)
         for t in range(TILES):
-            regroup(nc.scalar.copy, uout_grp, uout_raw, t * P, (t + 1) * P)
-        quantise(nc, uout_codes, uout_scales, uout_grp, 0, CH)
+            nc.gpsimd.tensor_scalar(
+                out=uout_grp[:, t * P : (t + 1) * P, :],
+                in0=uout_raw[:, :, t * P : (t + 1) * P].rearrange("p j c -> p c j"),
+                scalar1=1.0,
+                scalar2=0.0,
+                op0=MULT,
+                op1=ADD,
+            )
 
-        y1 = keep.tile([P, TILES, POS], F32)
-        y2 = keep.tile([P, TILES, POS], F32)
-        side = keep.tile([P, TILES, POS], F32)
-        y3 = keep.tile([P, TILES, POS], BF16)
-        nc.vector.memset(side[:].rearrange("p t (m d) -> p (t m) d", d=D)[:, :, 0:1], 0.0)
+        def scale_by_tap(dst, src, coef):
+            nc.scalar.activation(out=dst, in_=src, func=COPY, scale=coef)
 
         def add_tap(acc, src, coef):
             nc.vector.scalar_tensor_tensor(out=acc, in0=src, scalar=coef, in1=acc, op0=MULT, op1=ADD)
 
         step = W * D
-        for t in range(TILES):
-            nc.scalar.activation(out=y1[:, t, :], in_=y0[t][:, 0:POS], func=COPY, scale=tap(0, 1, t))
-        for t in range(TILES):
-            add_tap(y1[:, t, step:POS], y0[t][:, 0 : POS - step], tap(0, 0, t))
-        for t in range(TILES):
-            add_tap(y1[:, t, 0 : POS - step], y0[t][:, step:POS], tap(0, 2, t))
+        for pair in PAIRS:
+            for t in pair:
+                scale_by_tap(y1[:, t, :], y0[t][:, 0:POS], tap(0, 1, t))
+            for t in pair:
+                add_tap(y1[:, t, step:POS], y0[t][:, 0 : POS - step], tap(0, 0, t))
+            for t in pair:
+                add_tap(y1[:, t, 0 : POS - step], y0[t][:, step:POS], tap(0, 2, t))
 
-        for t in range(TILES):
-            nc.scalar.activation(out=y2[:, t, :], in_=y1[:, t, :], func=COPY, scale=tap(1, 1, t))
-        for t in range(TILES):
-            src = y1[:, t, :].rearrange("p (h n) -> p h n", n=step)
-            acc = y2[:, t, :].rearrange("p (h n) -> p h n", n=step)
-            add_tap(acc[:, :, D:step], src[:, :, 0 : step - D], tap(1, 0, t))
-        for t in range(TILES):
-            src = y1[:, t, :].rearrange("p (h n) -> p h n", n=step)
-            acc = y2[:, t, :].rearrange("p (h n) -> p h n", n=step)
-            add_tap(acc[:, :, 0 : step - D], src[:, :, D:step], tap(1, 2, t))
+        for pair in PAIRS:
+            for t in pair:
+                scale_by_tap(y2[:, t, :], y1[:, t, :], tap(1, 1, t))
+            for t in pair:
+                src = y1[:, t, :].rearrange("p (h n) -> p h n", n=step)
+                acc = y2[:, t, :].rearrange("p (h n) -> p h n", n=step)
+                add_tap(acc[:, :, D:step], src[:, :, 0 : step - D], tap(1, 0, t))
+            for t in pair:
+                src = y1[:, t, :].rearrange("p (h n) -> p h n", n=step)
+                acc = y2[:, t, :].rearrange("p (h n) -> p h n", n=step)
+                add_tap(acc[:, :, 0 : step - D], src[:, :, D:step], tap(1, 2, t))
+
+        quantise(nc, uout_codes, uout_scales, uout_grp, 0, CH)
+
+        for pair in PAIRS:
+            for t in pair:
+                src = y2[:, t, :].rearrange("p (m d) -> p m d", d=D)
+                acc = side[:, t, :].rearrange("p (m d) -> p m d", d=D)
+                scale_by_tap(acc[:, :, 1:D], src[:, :, 0 : D - 1], tap(2, 0, t))
+            for t in pair:
+                src = y2[:, t, :].rearrange("p (m d) -> p m d", d=D)
+                acc = side[:, t, :].rearrange("p (m d) -> p m d", d=D)
+                add_tap(acc[:, :, 0 : D - 1], src[:, :, 1:D], tap(2, 2, t))
 
         y3_grp = keep.tile([P, POS, PACK], BF16, align_bytes=64)
         y3_codes = keep.tile([P, POS], U32, align_bytes=64)
         y3_scales = keep.tile([P, POS], U8, align_bytes=64)
-        res = keep.tile([P, TILES, POS], F32)
-        o_ps = [psum.tile([P, 512], F32, tag="bank", name="o_%d" % t) for t in range(TILES)]
-        out_view = out_rows.rearrange("(t p) n -> p t n", p=P)
         for lo, hi in CHUNKS:
-            for t in range(TILES):
-                src = y2[:, t, lo:hi].rearrange("p (m d) -> p m d", d=D)
-                acc = side[:, t, lo:hi].rearrange("p (m d) -> p m d", d=D)
-                nc.scalar.activation(
-                    out=acc[:, :, 1:D], in_=src[:, :, 0 : D - 1], func=COPY, scale=tap(2, 0, t)
-                )
-            for t in range(TILES):
-                src = y2[:, t, lo:hi].rearrange("p (m d) -> p m d", d=D)
-                acc = side[:, t, lo:hi].rearrange("p (m d) -> p m d", d=D)
-                add_tap(acc[:, :, 0 : D - 1], src[:, :, 1:D], tap(2, 2, t))
             for t in range(TILES):
                 nc.vector.scalar_tensor_tensor(
                     out=y3[:, t, lo:hi],
@@ -172,22 +185,20 @@ def tile_lowrankconv3d_s_kernel(tc, x, U_kh, U_kw, U_kd, U_c_in, U_c_out, bias, 
                     op0=MULT,
                     op1=ADD,
                 )
-            last = hi == POS
-            regroup(nc.vector.tensor_copy if last else nc.scalar.copy, y3_grp, y3, lo, hi)
+        regroup(nc.scalar.copy, y3_grp, y3, 0, 256)
+        regroup(nc.vector.tensor_copy, y3_grp, y3, 256, 384)
+
+        res = keep.tile([P, TILES, POS], F32)
+        o_ps = [psum.tile([P, 512], F32, tag="bank", name="o_%d" % t) for t in range(TILES)]
+        out_view = out_rows.rearrange("(t p) n -> p t n", p=P)
+        for lo, hi in CHUNKS:
             quantise(nc, y3_codes, y3_scales, y3_grp, lo, hi)
             for t in range(TILES):
-                nc.tensor.matmul_mx(
-                    out=o_ps[t][:, lo:hi],
-                    lhsT=uout_codes[:, t * P : (t + 1) * P].bitcast(FP8X4),
-                    lhsT_scale=uout_scales[:, t * P : (t + 1) * P],
-                    rhs=y3_codes[:, lo:hi].bitcast(FP8X4),
-                    rhs_scale=y3_scales[:, lo:hi],
-                    start=True,
-                    stop=True,
-                )
+                product(nc, o_ps[t], uout_codes, uout_scales, t, y3_codes, y3_scales, lo, hi)
+        for lo, hi in CHUNKS:
             for t in range(TILES):
                 bias_t = par[:, bias_row + t : bias_row + t + 1]
-                if t % 2 == 0 or not last:
+                if t % 2 == 0:
                     nc.scalar.activation(
                         out=res[:, t, lo:hi], in_=o_ps[t][:, lo:hi], func=IDENTITY, bias=bias_t
                     )

@@ -43,7 +43,7 @@ def quantise(nc, codes, scales, grouped, lo, hi):
 
 def product(nc, bank, w_codes, w_scales, t, m_codes, m_scales, lo, hi):
     nc.tensor.matmul_mx(
-        out=bank[:, lo:hi],
+        out=bank,
         lhsT=w_codes[:, t * P : (t + 1) * P].bitcast(FP8X4),
         lhsT_scale=w_scales[:, t * P : (t + 1) * P],
         rhs=m_codes[:, lo:hi].bitcast(FP8X4),
@@ -66,9 +66,10 @@ def tile_lowrankconv3d_s_kernel(tc, x, U_kh, U_kw, U_kd, U_c_in, U_c_out, bias, 
         x_raw = keep.tile([P, PACK, POS], BF16)
         uin_raw = keep.tile([P, PACK, CH], BF16)
         uout_raw = keep.tile([P, PACK, CH], BF16)
-        nc.sync.dma_start(out=x_raw[:], in_=x_rows.rearrange("(p j) n -> p j n", j=PACK))
+        x_view = x_rows.rearrange("(p j) n -> p j n", j=PACK)
         uin_view = U_c_in.rearrange("(p j) r -> p j r", j=PACK)
         half = CH // 2
+        nc.sync.dma_start(out=x_raw[:], in_=x_view)
         nc.sync.dma_start(out=uin_raw[:, :, 0:half], in_=uin_view[:, :, 0:half])
         nc.sync.dma_start(out=uin_raw[:, :, half:CH], in_=uin_view[:, :, half:CH])
         nc.sync.dma_start(out=uout_raw[:], in_=U_c_out.rearrange("(t p) o -> p t o", p=P))
@@ -89,7 +90,6 @@ def tile_lowrankconv3d_s_kernel(tc, x, U_kh, U_kw, U_kd, U_c_in, U_c_out, bias, 
         par_ps = psum.tile([P, P], BF16, tag="bank")
         nc.tensor.transpose(par_ps[:], par_rows[:], ident[:])
         par = keep.tile([P, bias_row + TILES], F32)
-        nc.scalar.activation(out=par[:], in_=par_ps[:, 0 : bias_row + TILES], func=COPY)
 
         def tap(f, k, t):
             col = (f * TAPS + k) * TILES + t
@@ -107,18 +107,20 @@ def tile_lowrankconv3d_s_kernel(tc, x, U_kh, U_kw, U_kd, U_c_in, U_c_out, bias, 
         uin_grp = keep.tile([P, CH, PACK], BF16, align_bytes=64)
         uin_codes = keep.tile([P, CH], U32, align_bytes=64)
         uin_scales = keep.tile([P, CH], U8, align_bytes=64)
+        y0 = [psum.tile([P, 512], F32, tag="bank", name="y0_%d" % t) for t in range(TILES)]
         regroup(nc.vector.tensor_copy, x_grp, x_raw, 0, 256)
         regroup(nc.scalar.copy, x_grp, x_raw, 256, 384)
         regroup(nc.vector.tensor_copy, uin_grp, uin_raw, 0, half)
         regroup(nc.scalar.copy, uin_grp, uin_raw, half, CH)
         quantise(nc, x_codes, x_scales, x_grp, 0, 256)
         quantise(nc, x_codes, x_scales, x_grp, 256, 384)
-        y0 = [psum.tile([P, 512], F32, tag="bank", name="y0_%d" % t) for t in range(TILES)]
         for pair in PAIRS:
             quantise(nc, uin_codes, uin_scales, uin_grp, pair[0] * P, (pair[1] + 1) * P)
             for t in pair:
                 for lo, hi in CHUNKS:
-                    product(nc, y0[t], uin_codes, uin_scales, t, x_codes, x_scales, lo, hi)
+                    product(nc, y0[t][:, lo:hi], uin_codes, uin_scales, t, x_codes, x_scales, lo, hi)
+
+        nc.scalar.activation(out=par[:], in_=par_ps[:, 0 : bias_row + TILES], func=COPY)
 
         uout_grp = keep.tile([P, CH, PACK], BF16, align_bytes=64)
         uout_codes = keep.tile([P, CH], U32, align_bytes=64)
@@ -148,34 +150,30 @@ def tile_lowrankconv3d_s_kernel(tc, x, U_kh, U_kw, U_kd, U_c_in, U_c_out, bias, 
             for t in pair:
                 add_tap(y1[:, t, 0 : POS - step], y0[t][:, step:POS], tap(0, 2, t))
 
-        for pair in PAIRS:
-            for t in pair:
-                scale_by_tap(y2[:, t, :], y1[:, t, :], tap(1, 1, t))
-            for t in pair:
-                src = y1[:, t, :].rearrange("p (h n) -> p h n", n=step)
-                acc = y2[:, t, :].rearrange("p (h n) -> p h n", n=step)
-                add_tap(acc[:, :, D:step], src[:, :, 0 : step - D], tap(1, 0, t))
-            for t in pair:
-                src = y1[:, t, :].rearrange("p (h n) -> p h n", n=step)
-                acc = y2[:, t, :].rearrange("p (h n) -> p h n", n=step)
-                add_tap(acc[:, :, 0 : step - D], src[:, :, D:step], tap(1, 2, t))
+        def w_taps(lo, hi):
+            for pair in PAIRS:
+                for t in pair:
+                    src = y1[:, t, lo:hi].rearrange("p (h n) -> p h n", n=step)
+                    acc = y2[:, t, lo:hi].rearrange("p (h n) -> p h n", n=step)
+                    add_tap(acc[:, :, D:step], src[:, :, 0 : step - D], tap(1, 0, t))
+                for t in pair:
+                    src = y1[:, t, lo:hi].rearrange("p (h n) -> p h n", n=step)
+                    acc = y2[:, t, lo:hi].rearrange("p (h n) -> p h n", n=step)
+                    add_tap(acc[:, :, 0 : step - D], src[:, :, D:step], tap(1, 2, t))
 
-        quantise(nc, uout_codes, uout_scales, uout_grp, 0, CH)
-
-        for pair in PAIRS:
-            for t in pair:
-                src = y2[:, t, :].rearrange("p (m d) -> p m d", d=D)
-                acc = side[:, t, :].rearrange("p (m d) -> p m d", d=D)
+        def d_low_tap(lo, hi):
+            for t in range(TILES):
+                src = y2[:, t, lo:hi].rearrange("p (m d) -> p m d", d=D)
+                acc = side[:, t, lo:hi].rearrange("p (m d) -> p m d", d=D)
                 scale_by_tap(acc[:, :, 1:D], src[:, :, 0 : D - 1], tap(2, 0, t))
-            for t in pair:
-                src = y2[:, t, :].rearrange("p (m d) -> p m d", d=D)
-                acc = side[:, t, :].rearrange("p (m d) -> p m d", d=D)
+
+        def d_high_tap(lo, hi):
+            for t in range(TILES):
+                src = y2[:, t, lo:hi].rearrange("p (m d) -> p m d", d=D)
+                acc = side[:, t, lo:hi].rearrange("p (m d) -> p m d", d=D)
                 add_tap(acc[:, :, 0 : D - 1], src[:, :, 1:D], tap(2, 2, t))
 
-        y3_grp = keep.tile([P, POS, PACK], BF16, align_bytes=64)
-        y3_codes = keep.tile([P, POS], U32, align_bytes=64)
-        y3_scales = keep.tile([P, POS], U8, align_bytes=64)
-        for lo, hi in CHUNKS:
+        def d_centre_tap(lo, hi):
             for t in range(TILES):
                 nc.vector.scalar_tensor_tensor(
                     out=y3[:, t, lo:hi],
@@ -185,23 +183,49 @@ def tile_lowrankconv3d_s_kernel(tc, x, U_kh, U_kw, U_kd, U_c_in, U_c_out, bias, 
                     op0=MULT,
                     op1=ADD,
                 )
-        regroup(nc.scalar.copy, y3_grp, y3, 0, 256)
-        regroup(nc.vector.tensor_copy, y3_grp, y3, 256, 384)
 
+        for t in range(TILES):
+            scale_by_tap(y2[:, t, :], y1[:, t, :], tap(1, 1, t))
+        w_taps(0, POS)
+        d_low_tap(0, POS)
+        y3_grp = keep.tile([P, POS, PACK], BF16, align_bytes=64)
+        y3_codes = keep.tile([P, POS], U32, align_bytes=64)
+        y3_scales = keep.tile([P, POS], U8, align_bytes=64)
         res = keep.tile([P, TILES, POS], F32)
-        o_ps = [psum.tile([P, 512], F32, tag="bank", name="o_%d" % t) for t in range(TILES)]
         out_view = out_rows.rearrange("(t p) n -> p t n", p=P)
-        for lo, hi in CHUNKS:
-            quantise(nc, y3_codes, y3_scales, y3_grp, lo, hi)
+
+        def second_product(lo, hi):
+            banks = [psum.tile([P, 512], F32, tag="bank", name="o_%d_%d" % (lo, t)) for t in range(TILES)]
             for t in range(TILES):
-                product(nc, o_ps[t], uout_codes, uout_scales, t, y3_codes, y3_scales, lo, hi)
-        for lo, hi in CHUNKS:
-            for t in range(TILES):
-                bias_t = par[:, bias_row + t : bias_row + t + 1]
-                if t % 2 == 0:
-                    nc.scalar.activation(
-                        out=res[:, t, lo:hi], in_=o_ps[t][:, lo:hi], func=IDENTITY, bias=bias_t
-                    )
-                else:
-                    nc.vector.tensor_scalar_add(out=res[:, t, lo:hi], in0=o_ps[t][:, lo:hi], scalar1=bias_t)
-            nc.sync.dma_start(out=out_view[:, :, lo:hi], in_=res[:, :, lo:hi])
+                product(nc, banks[t][:, 0 : hi - lo], uout_codes, uout_scales, t, y3_codes, y3_scales, lo, hi)
+            return banks
+
+        def add_bias(banks, t, lo, hi, on_scalar):
+            bias_t = par[:, bias_row + t : bias_row + t + 1]
+            if on_scalar:
+                nc.scalar.activation(
+                    out=res[:, t, lo:hi], in_=banks[t][:, 0 : hi - lo], func=IDENTITY, bias=bias_t
+                )
+            else:
+                nc.vector.tensor_scalar_add(out=res[:, t, lo:hi], in0=banks[t][:, 0 : hi - lo], scalar1=bias_t)
+
+        d_high_tap(0, 256)
+        d_centre_tap(0, 256)
+        regroup(nc.scalar.copy, y3_grp, y3, 0, 256)
+        quantise(nc, uout_codes, uout_scales, uout_grp, 0, CH)
+        d_high_tap(256, POS)
+        quantise(nc, y3_codes, y3_scales, y3_grp, 0, 256)
+        banks_a = second_product(0, 256)
+        d_centre_tap(256, POS)
+        regroup(nc.vector.tensor_copy, y3_grp, y3, 256, POS)
+        quantise(nc, y3_codes, y3_scales, y3_grp, 256, POS)
+        banks_b = second_product(256, POS)
+        for pair in PAIRS:
+            for t in pair:
+                add_bias(banks_a, t, 0, 256, True)
+            nc.sync.dma_start(
+                out=out_view[:, pair[0] : pair[1] + 1, 0:256], in_=res[:, pair[0] : pair[1] + 1, 0:256]
+            )
+        for t in range(TILES):
+            add_bias(banks_b, t, 256, POS, False)
+        nc.sync.dma_start(out=out_view[:, :, 256:POS], in_=res[:, :, 256:POS])

@@ -125,15 +125,7 @@ def tile_lowrankconv3d_s_kernel(tc, x, U_kh, U_kw, U_kd, U_c_in, U_c_out, bias, 
         uout_grp = keep.tile([P, CH, PACK], BF16, align_bytes=64)
         uout_codes = keep.tile([P, CH], U32, align_bytes=64)
         uout_scales = keep.tile([P, CH], U8, align_bytes=64)
-        for t in range(TILES):
-            nc.gpsimd.tensor_scalar(
-                out=uout_grp[:, t * P : (t + 1) * P, :],
-                in0=uout_raw[:, :, t * P : (t + 1) * P].rearrange("p j c -> p c j"),
-                scalar1=1.0,
-                scalar2=0.0,
-                op0=MULT,
-                op1=ADD,
-            )
+        regroup(nc.vector.tensor_copy, uout_grp, uout_raw, 0, CH)
 
         def scale_by_tap(dst, src, coef):
             nc.scalar.activation(out=dst, in_=src, func=COPY, scale=coef)

@@ -74,26 +74,28 @@ def tile_lowrankconv3d_s_kernel(tc, x, U_kh, U_kw, U_kd, U_c_in, U_c_out, bias, 
         nc.sync.dma_start(out=uin_raw[:, :, half:CH], in_=uin_view[:, :, half:CH])
         nc.sync.dma_start(out=uout_raw[:], in_=U_c_out.rearrange("(t p) o -> p t o", p=P))
 
-        par_rows = keep.tile([P, P], BF16)
-        nc.vector.memset(par_rows[:], 0.0)
+        par_rows = keep.tile([P, TAPS * P], BF16)
+        nc.gpsimd.memset(par_rows[:], 0.0)
         for f, taps in enumerate((U_kh, U_kw, U_kd)):
             nc.scalar.dma_start(
-                out=par_rows[f * TAPS * TILES : (f + 1) * TAPS * TILES, :],
-                in_=taps.rearrange("k (t p) -> (k t) p", p=P),
+                out=par_rows[f * TILES : (f + 1) * TILES, :],
+                in_=taps.rearrange("k r -> (k r)").rearrange("(q c) -> q c", q=TILES),
             )
-        bias_row = 3 * TAPS * TILES
+        bias_row = 3 * TILES
+        used_rows = bias_row + TILES
         nc.scalar.dma_start(
-            out=par_rows[bias_row : bias_row + TILES, :], in_=bias.rearrange("(t p) -> t p", p=P)
+            out=par_rows[bias_row:used_rows, 0:P], in_=bias.rearrange("(t p) -> t p", p=P)
         )
         ident = keep.tile([P, P], BF16)
         make_identity(nc, ident[:])
-        par_ps = psum.tile([P, P], BF16, tag="bank")
-        nc.tensor.transpose(par_ps[:], par_rows[:], ident[:])
-        par = keep.tile([P, bias_row + TILES], F32)
+        par_ps = psum.tile([P, TAPS, P], BF16, tag="bank")
+        for b in range(TAPS):
+            nc.tensor.transpose(par_ps[:, b, :], par_rows[:, b * P : (b + 1) * P], ident[:])
+        par = keep.tile([P, TAPS, used_rows], F32)
 
         def tap(f, k, t):
-            col = (f * TAPS + k) * TILES + t
-            return par[:, col : col + 1]
+            q, b = divmod(k * TILES + t, TAPS)
+            return par[:, b, f * TILES + q : f * TILES + q + 1]
 
         y1 = keep.tile([P, TILES, POS], F32)
         y2 = keep.tile([P, TILES, POS], F32)
@@ -120,7 +122,7 @@ def tile_lowrankconv3d_s_kernel(tc, x, U_kh, U_kw, U_kd, U_c_in, U_c_out, bias, 
                 for lo, hi in CHUNKS:
                     product(nc, y0[t][:, lo:hi], uin_codes, uin_scales, t, x_codes, x_scales, lo, hi)
 
-        nc.scalar.activation(out=par[:], in_=par_ps[:, 0 : bias_row + TILES], func=COPY)
+        nc.scalar.activation(out=par[:], in_=par_ps[:, :, 0:used_rows], func=COPY)
 
         uout_grp = keep.tile([P, CH, PACK], BF16, align_bytes=64)
         uout_codes = keep.tile([P, CH], U32, align_bytes=64)
@@ -193,7 +195,7 @@ def tile_lowrankconv3d_s_kernel(tc, x, U_kh, U_kw, U_kd, U_c_in, U_c_out, bias, 
             return banks
 
         def add_bias(banks, t, lo, hi, on_scalar):
-            bias_t = par[:, bias_row + t : bias_row + t + 1]
+            bias_t = par[:, 0, bias_row + t : bias_row + t + 1]
             if on_scalar:
                 nc.scalar.activation(
                     out=res[:, t, lo:hi], in_=banks[t][:, 0 : hi - lo], func=IDENTITY, bias=bias_t

@@ -70,22 +70,22 @@ def tile_lowrankconv3d_s_kernel(tc, x, U_kh, U_kw, U_kd, U_c_in, U_c_out, bias, 
         uin_view = U_c_in.rearrange("(p j) r -> p j r", j=PACK)
         half = CH // 2
         nc.sync.dma_start(out=x_raw[:], in_=x_view)
-        nc.sync.dma_start(out=uin_raw[:, :, 0:half], in_=uin_view[:, :, 0:half])
-        nc.sync.dma_start(out=uin_raw[:, :, half:CH], in_=uin_view[:, :, half:CH])
-        nc.sync.dma_start(out=uout_raw[:], in_=U_c_out.rearrange("(t p) o -> p t o", p=P))
 
         par_rows = keep.tile([P, TAPS * P], BF16)
         nc.gpsimd.memset(par_rows[:], 0.0)
         for f, taps in enumerate((U_kh, U_kw, U_kd)):
-            nc.scalar.dma_start(
+            nc.sync.dma_start(
                 out=par_rows[f * TILES : (f + 1) * TILES, :],
                 in_=taps.rearrange("k r -> (k r)").rearrange("(q c) -> q c", q=TILES),
             )
         bias_row = 3 * TILES
         used_rows = bias_row + TILES
-        nc.scalar.dma_start(
+        nc.sync.dma_start(
             out=par_rows[bias_row:used_rows, 0:P], in_=bias.rearrange("(t p) -> t p", p=P)
         )
+        nc.sync.dma_start(out=uin_raw[:, :, 0:half], in_=uin_view[:, :, 0:half])
+        nc.sync.dma_start(out=uin_raw[:, :, half:CH], in_=uin_view[:, :, half:CH])
+        nc.sync.dma_start(out=uout_raw[:], in_=U_c_out.rearrange("(t p) o -> p t o", p=P))
         ident = keep.tile([P, P], BF16)
         make_identity(nc, ident[:])
         par_ps = psum.tile([P, TAPS, P], BF16, tag="bank")
@@ -110,24 +110,30 @@ def tile_lowrankconv3d_s_kernel(tc, x, U_kh, U_kw, U_kd, U_c_in, U_c_out, bias, 
         uin_codes = keep.tile([P, CH], U32, align_bytes=64)
         uin_scales = keep.tile([P, CH], U8, align_bytes=64)
         y0 = [psum.tile([P, 512], F32, tag="bank", name="y0_%d" % t) for t in range(TILES)]
+        def first_product(t):
+            for lo, hi in CHUNKS:
+                product(nc, y0[t][:, lo:hi], uin_codes, uin_scales, t, x_codes, x_scales, lo, hi)
+
         regroup(nc.vector.tensor_copy, x_grp, x_raw, 0, 256)
         regroup(nc.scalar.copy, x_grp, x_raw, 256, 384)
-        regroup(nc.vector.tensor_copy, uin_grp, uin_raw, 0, half)
-        regroup(nc.scalar.copy, uin_grp, uin_raw, half, CH)
+        regroup(nc.scalar.copy, uin_grp, uin_raw, 0, P)
+        regroup(nc.vector.tensor_copy, uin_grp, uin_raw, P, 2 * P)
+        regroup(nc.scalar.copy, uin_grp, uin_raw, 2 * P, 3 * P)
+        nc.scalar.activation(out=par[:], in_=par_ps[:, :, 0:used_rows], func=COPY)
         quantise(nc, x_codes, x_scales, x_grp, 0, 256)
         quantise(nc, x_codes, x_scales, x_grp, 256, 384)
-        for pair in PAIRS:
-            quantise(nc, uin_codes, uin_scales, uin_grp, pair[0] * P, (pair[1] + 1) * P)
-            for t in pair:
-                for lo, hi in CHUNKS:
-                    product(nc, y0[t][:, lo:hi], uin_codes, uin_scales, t, x_codes, x_scales, lo, hi)
-
-        nc.scalar.activation(out=par[:], in_=par_ps[:, :, 0:used_rows], func=COPY)
+        quantise(nc, uin_codes, uin_scales, uin_grp, 0, P)
+        first_product(0)
+        regroup(nc.vector.tensor_copy, uin_grp, uin_raw, 3 * P, CH)
+        quantise(nc, uin_codes, uin_scales, uin_grp, P, 2 * P)
+        first_product(1)
+        quantise(nc, uin_codes, uin_scales, uin_grp, 2 * P, CH)
+        first_product(2)
+        first_product(3)
 
         uout_grp = keep.tile([P, CH, PACK], BF16, align_bytes=64)
         uout_codes = keep.tile([P, CH], U32, align_bytes=64)
         uout_scales = keep.tile([P, CH], U8, align_bytes=64)
-        regroup(nc.vector.tensor_copy, uout_grp, uout_raw, 0, CH)
 
         def scale_by_tap(dst, src, coef):
             nc.scalar.activation(out=dst, in_=src, func=COPY, scale=coef)
@@ -155,8 +161,8 @@ def tile_lowrankconv3d_s_kernel(tc, x, U_kh, U_kw, U_kd, U_c_in, U_c_out, bias, 
                     acc = y2[:, t, lo:hi].rearrange("p (h n) -> p h n", n=step)
                     add_tap(acc[:, :, 0 : step - D], src[:, :, D:step], tap(1, 2, t))
 
-        def d_low_tap(lo, hi):
-            for t in range(TILES):
+        def d_low_tap(lo, hi, tiles):
+            for t in tiles:
                 src = y2[:, t, lo:hi].rearrange("p (m d) -> p m d", d=D)
                 acc = side[:, t, lo:hi].rearrange("p (m d) -> p m d", d=D)
                 scale_by_tap(acc[:, :, 1:D], src[:, :, 0 : D - 1], tap(2, 0, t))
@@ -178,10 +184,14 @@ def tile_lowrankconv3d_s_kernel(tc, x, U_kh, U_kw, U_kd, U_c_in, U_c_out, bias, 
                     op1=ADD,
                 )
 
-        for t in range(TILES):
-            scale_by_tap(y2[:, t, :], y1[:, t, :], tap(1, 1, t))
+        for pair in PAIRS:
+            regroup(nc.scalar.copy, uout_grp, uout_raw, pair[0] // 2 * P, (pair[0] // 2 + 1) * P)
+            for t in pair:
+                scale_by_tap(y2[:, t, :], y1[:, t, :], tap(1, 1, t))
         w_taps(0, POS)
-        d_low_tap(0, POS)
+        for pair in PAIRS:
+            d_low_tap(0, POS, pair)
+            regroup(nc.scalar.copy, uout_grp, uout_raw, (2 + pair[0] // 2) * P, (3 + pair[0] // 2) * P)
         y3_grp = keep.tile([P, POS, PACK], BF16, align_bytes=64)
         y3_codes = keep.tile([P, POS], U32, align_bytes=64)
         y3_scales = keep.tile([P, POS], U8, align_bytes=64)

@@ -230,6 +230,9 @@ def tile_lowrankconv3d_s_kernel(tc, x, U_kh, U_kw, U_kd, U_c_in, U_c_out, bias, 
             nc.sync.dma_start(
                 out=out_view[:, pair[0] : pair[1] + 1, 0:256], in_=res[:, pair[0] : pair[1] + 1, 0:256]
             )
-        for t in range(TILES):
-            add_bias(banks_b, t, 256, POS, False)
-        nc.sync.dma_start(out=out_view[:, :, 256:POS], in_=res[:, :, 256:POS])
+        for pair in PAIRS:
+            for t in pair:
+                add_bias(banks_b, t, 256, POS, False)
+            nc.sync.dma_start(
+                out=out_view[:, pair[0] : pair[1] + 1, 256:POS], in_=res[:, pair[0] : pair[1] + 1, 256:POS]
+            )

@@ -70,6 +70,7 @@ def tile_lowrankconv3d_s_kernel(tc, x, U_kh, U_kw, U_kd, U_c_in, U_c_out, bias, 
         uin_view = U_c_in.rearrange("(p j) r -> p j r", j=PACK)
         half = CH // 2
         nc.sync.dma_start(out=x_raw[:], in_=x_view)
+        nc.sync.dma_start(out=uin_raw[:, :, 0:half], in_=uin_view[:, :, 0:half])
 
         par_rows = keep.tile([P, TAPS * P], BF16)
         nc.gpsimd.memset(par_rows[:], 0.0)
@@ -83,7 +84,6 @@ def tile_lowrankconv3d_s_kernel(tc, x, U_kh, U_kw, U_kd, U_c_in, U_c_out, bias, 
         nc.sync.dma_start(
             out=par_rows[bias_row:used_rows, 0:P], in_=bias.rearrange("(t p) -> t p", p=P)
         )
-        nc.sync.dma_start(out=uin_raw[:, :, 0:half], in_=uin_view[:, :, 0:half])
         nc.sync.dma_start(out=uin_raw[:, :, half:CH], in_=uin_view[:, :, half:CH])
         nc.sync.dma_start(out=uout_raw[:], in_=U_c_out.rearrange("(t p) o -> p t o", p=P))
         ident = keep.tile([P, P], BF16)

from contextlib import ExitStack

import concourse.mybir as mybir
from concourse.masks import make_identity

F32 = mybir.dt.float32
BF16 = mybir.dt.bfloat16
U32 = mybir.dt.uint32
U8 = mybir.dt.uint8
FP8X4 = mybir.dt.float8_e4m3fn_x4
MULT = mybir.AluOpType.mult
ADD = mybir.AluOpType.add
COPY = mybir.ActivationFunctionType.Copy
IDENTITY = mybir.ActivationFunctionType.Identity

P = 128
PACK = 4
CH = P * PACK
H, W, D = 6, 8, 8
POS = H * W * D
TAPS = 3
TILES = CH // P
CHUNKS = ((0, 256), (256, 384))
PAIRS = ((0, 1), (2, 3))

FLOPS = 2 * (2 * CH * CH * POS) + 3 * (2 * TAPS - 1) * CH * POS + CH * POS


def regroup(engine_copy, grouped, rows, lo, hi):
    engine_copy(
        out=grouped[:, lo:hi, :].rearrange("p (c i) j -> p c j i", i=4),
        in_=rows[:, :, lo:hi].rearrange("p j (c i) -> p c j i", i=4),
    )


def quantise(nc, codes, scales, grouped, lo, hi):
    nc.vector.quantize_mx(
        out=codes[:, lo:hi].bitcast(FP8X4),
        scales=scales[:, lo:hi],
        in_=grouped[:, lo:hi, :].rearrange("p c j -> p (c j)"),
    )


def product(nc, bank, w_codes, w_scales, t, m_codes, m_scales, lo, hi):
    nc.tensor.matmul_mx(
        out=bank,
        lhsT=w_codes[:, t * P : (t + 1) * P].bitcast(FP8X4),
        lhsT_scale=w_scales[:, t * P : (t + 1) * P],
        rhs=m_codes[:, lo:hi].bitcast(FP8X4),
        rhs_scale=m_scales[:, lo:hi],
        start=True,
        stop=True,
    )


def tile_lowrankconv3d_s_kernel(tc, x, U_kh, U_kw, U_kd, U_c_in, U_c_out, bias, out):
    nc = tc.nc
    x_rows = x.rearrange("b c h w d -> (b c) (h w d)")
    out_rows = out.rearrange("b o h w d -> (b o) (h w d)")

    with ExitStack() as stack:
        keep = stack.enter_context(tc.tile_pool(name="keep", bufs=1))
        psum = stack.enter_context(tc.psum_pool(name="psum", bufs=8))
        stack.enter_context(tc.manual_schedule())

        x_raw = keep.tile([P, PACK, POS], BF16)
        uin_raw = keep.tile([P, PACK, CH], BF16)
        uout_raw = keep.tile([P, PACK, CH], BF16)
        x_view = x_rows.rearrange("(p j) n -> p j n", j=PACK)
        uin_view = U_c_in.rearrange("(p j) r -> p j r", j=PACK)
        half = CH // 2
        nc.sync.dma_start(out=x_raw[:], in_=x_view)
        nc.sync.dma_start(out=uin_raw[:, :, 0:half], in_=uin_view[:, :, 0:half])

        par_rows = keep.tile([P, TAPS * P], BF16)
        nc.gpsimd.memset(par_rows[:], 0.0)
        for f, taps in enumerate((U_kh, U_kw, U_kd)):
            nc.sync.dma_start(
                out=par_rows[f * TILES : (f + 1) * TILES, :],
                in_=taps.rearrange("k r -> (k r)").rearrange("(q c) -> q c", q=TILES),
            )
        bias_row = 3 * TILES
        used_rows = bias_row + TILES
        nc.sync.dma_start(
            out=par_rows[bias_row:used_rows, 0:P], in_=bias.rearrange("(t p) -> t p", p=P)
        )
        nc.sync.dma_start(out=uin_raw[:, :, half:CH], in_=uin_view[:, :, half:CH])
        nc.sync.dma_start(out=uout_raw[:], in_=U_c_out.rearrange("(t p) o -> p t o", p=P))
        ident = keep.tile([P, P], BF16)
        make_identity(nc, ident[:])
        par_ps = psum.tile([P, TAPS, P], BF16, tag="bank")
        for b in range(TAPS):
            nc.tensor.transpose(par_ps[:, b, :], par_rows[:, b * P : (b + 1) * P], ident[:])
        par = keep.tile([P, TAPS, used_rows], F32)

        def tap(f, k, t):
            q, b = divmod(k * TILES + t, TAPS)
            return par[:, b, f * TILES + q : f * TILES + q + 1]

        y1 = keep.tile([P, TILES, POS], F32)
        y2 = keep.tile([P, TILES, POS], F32)
        side = keep.tile([P, TILES, POS], F32)
        y3 = keep.tile([P, TILES, POS], BF16)
        nc.vector.memset(side[:].rearrange("p t (m d) -> p (t m) d", d=D)[:, :, 0:1], 0.0)

        x_grp = keep.tile([P, POS, PACK], BF16, align_bytes=64)
        x_codes = keep.tile([P, POS], U32, align_bytes=64)
        x_scales = keep.tile([P, POS], U8, align_bytes=64)
        uin_grp = keep.tile([P, CH, PACK], BF16, align_bytes=64)
        uin_codes = keep.tile([P, CH], U32, align_bytes=64)
        uin_scales = keep.tile([P, CH], U8, align_bytes=64)
        y0 = [psum.tile([P, 512], F32, tag="bank", name="y0_%d" % t) for t in range(TILES)]
        def first_product(t):
            for lo, hi in CHUNKS:
                product(nc, y0[t][:, lo:hi], uin_codes, uin_scales, t, x_codes, x_scales, lo, hi)

        regroup(nc.vector.tensor_copy, x_grp, x_raw, 0, 256)
        regroup(nc.scalar.copy, x_grp, x_raw, 256, 384)
        regroup(nc.scalar.copy, uin_grp, uin_raw, 0, P)
        regroup(nc.vector.tensor_copy, uin_grp, uin_raw, P, 2 * P)
        regroup(nc.scalar.copy, uin_grp, uin_raw, 2 * P, 3 * P)
        nc.scalar.activation(out=par[:], in_=par_ps[:, :, 0:used_rows], func=COPY)
        quantise(nc, x_codes, x_scales, x_grp, 0, 256)
        quantise(nc, x_codes, x_scales, x_grp, 256, 384)
        quantise(nc, uin_codes, uin_scales, uin_grp, 0, P)
        first_product(0)
        regroup(nc.vector.tensor_copy, uin_grp, uin_raw, 3 * P, CH)
        quantise(nc, uin_codes, uin_scales, uin_grp, P, 2 * P)
        first_product(1)
        quantise(nc, uin_codes, uin_scales, uin_grp, 2 * P, CH)
        first_product(2)
        first_product(3)

        uout_grp = keep.tile([P, CH, PACK], BF16, align_bytes=64)
        uout_codes = keep.tile([P, CH], U32, align_bytes=64)
        uout_scales = keep.tile([P, CH], U8, align_bytes=64)

        def scale_by_tap(dst, src, coef):
            nc.scalar.activation(out=dst, in_=src, func=COPY, scale=coef)

        def add_tap(acc, src, coef):
            nc.vector.scalar_tensor_tensor(out=acc, in0=src, scalar=coef, in1=acc, op0=MULT, op1=ADD)

        step = W * D
        for pair in PAIRS:
            for t in pair:
                scale_by_tap(y1[:, t, :], y0[t][:, 0:POS], tap(0, 1, t))
            for t in pair:
                add_tap(y1[:, t, step:POS], y0[t][:, 0 : POS - step], tap(0, 0, t))
            for t in pair:
                add_tap(y1[:, t, 0 : POS - step], y0[t][:, step:POS], tap(0, 2, t))

        def w_taps(lo, hi):
            for pair in PAIRS:
                for t in pair:
                    src = y1[:, t, lo:hi].rearrange("p (h n) -> p h n", n=step)
                    acc = y2[:, t, lo:hi].rearrange("p (h n) -> p h n", n=step)
                    add_tap(acc[:, :, D:step], src[:, :, 0 : step - D], tap(1, 0, t))
                for t in pair:
                    src = y1[:, t, lo:hi].rearrange("p (h n) -> p h n", n=step)
                    acc = y2[:, t, lo:hi].rearrange("p (h n) -> p h n", n=step)
                    add_tap(acc[:, :, 0 : step - D], src[:, :, D:step], tap(1, 2, t))

        def d_low_tap(lo, hi, tiles):
            for t in tiles:
                src = y2[:, t, lo:hi].rearrange("p (m d) -> p m d", d=D)
                acc = side[:, t, lo:hi].rearrange("p (m d) -> p m d", d=D)
                scale_by_tap(acc[:, :, 1:D], src[:, :, 0 : D - 1], tap(2, 0, t))

        def d_high_tap(lo, hi):
            for t in range(TILES):
                src = y2[:, t, lo:hi].rearrange("p (m d) -> p m d", d=D)
                acc = side[:, t, lo:hi].rearrange("p (m d) -> p m d", d=D)
                add_tap(acc[:, :, 0 : D - 1], src[:, :, 1:D], tap(2, 2, t))

        def d_centre_tap(lo, hi):
            for t in range(TILES):
                nc.vector.scalar_tensor_tensor(
                    out=y3[:, t, lo:hi],
                    in0=y2[:, t, lo:hi],
                    scalar=tap(2, 1, t),
                    in1=side[:, t, lo:hi],
                    op0=MULT,
                    op1=ADD,
                )

        for pair in PAIRS:
            regroup(nc.scalar.copy, uout_grp, uout_raw, pair[0] // 2 * P, (pair[0] // 2 + 1) * P)
            for t in pair:
                scale_by_tap(y2[:, t, :], y1[:, t, :], tap(1, 1, t))
        w_taps(0, POS)
        for pair in PAIRS:
            d_low_tap(0, POS, pair)
            regroup(nc.scalar.copy, uout_grp, uout_raw, (2 + pair[0] // 2) * P, (3 + pair[0] // 2) * P)
        y3_grp = keep.tile([P, POS, PACK], BF16, align_bytes=64)
        y3_codes = keep.tile([P, POS], U32, align_bytes=64)
        y3_scales = keep.tile([P, POS], U8, align_bytes=64)
        res = keep.tile([P, TILES, POS], F32)
        out_view = out_rows.rearrange("(t p) n -> p t n", p=P)

        def second_product(lo, hi):
            banks = [psum.tile([P, 512], F32, tag="bank", name="o_%d_%d" % (lo, t)) for t in range(TILES)]
            for t in range(TILES):
                product(nc, banks[t][:, 0 : hi - lo], uout_codes, uout_scales, t, y3_codes, y3_scales, lo, hi)
            return banks

        def add_bias(banks, t, lo, hi, on_scalar):
            bias_t = par[:, 0, bias_row + t : bias_row + t + 1]
            if on_scalar:
                nc.scalar.activation(
                    out=res[:, t, lo:hi], in_=banks[t][:, 0 : hi - lo], func=IDENTITY, bias=bias_t
                )
            else:
                nc.vector.tensor_scalar_add(out=res[:, t, lo:hi], in0=banks[t][:, 0 : hi - lo], scalar1=bias_t)

        d_high_tap(0, 256)
        d_centre_tap(0, 256)
        regroup(nc.scalar.copy, y3_grp, y3, 0, 256)
        quantise(nc, uout_codes, uout_scales, uout_grp, 0, CH)
        d_high_tap(256, POS)
        quantise(nc, y3_codes, y3_scales, y3_grp, 0, 256)
        banks_a = second_product(0, 256)
        d_centre_tap(256, POS)
        regroup(nc.vector.tensor_copy, y3_grp, y3, 256, POS)
        quantise(nc, y3_codes, y3_scales, y3_grp, 256, POS)
        banks_b = second_product(256, POS)
        for pair in PAIRS:
            for t in pair:
                add_bias(banks_a, t, 0, 256, True)
            nc.sync.dma_start(
                out=out_view[:, pair[0] : pair[1] + 1, 0:256], in_=res[:, pair[0] : pair[1] + 1, 0:256]
            )
        for pair in PAIRS:
            for t in pair:
                add_bias(banks_b, t, 256, POS, False)
            nc.sync.dma_start(
                out=out_view[:, pair[0] : pair[1] + 1, 256:POS], in_=res[:, pair[0] : pair[1] + 1, 256:POS]
            )
